import numpy as np
import ml_dtypes


def mxq(x, axis, fmt="e4m3"):
    dtype, down = {"e4m3": (ml_dtypes.float8_e4m3fn, 7), "e5m2": (ml_dtypes.float8_e5m2, 14)}[fmt]
    v = np.moveaxis(np.asarray(x, np.float32).astype(ml_dtypes.bfloat16).astype(np.float64), axis, -1)
    blocks = v.reshape(v.shape[:-1] + (-1, 32))
    amax = np.abs(blocks).max(-1, keepdims=True)
    byte = np.maximum(np.where(amax > 0, np.frexp(amax)[1] - 1 + 127, 0) - down, 1)
    scale = np.exp2(byte - 127.0)
    codes = (blocks / scale).astype(np.float32).astype(dtype).astype(np.float64)
    return np.moveaxis((codes * scale).reshape(v.shape), -1, axis)


WIDE = False


def mx_kscale(k):
    if not WIDE:
        return np.ones(k)
    levels = np.array([10, -10, 5, -5, 0])
    a = np.random.permutation(np.resize(levels, k // 512 * 4)).reshape(k // 512, 4)
    idx = np.arange(k)
    return np.exp2(a[idx // 512, idx % 128 // 32])


BF16 = ml_dtypes.bfloat16


def bf(x):
    return np.asarray(x, np.float32).astype(BF16)


def f64(x):
    return np.asarray(x).astype(np.float64)


B, H, T, D = 8, 1, 512, 1024
QS = 0.7 / D ** 0.25
VS = 4.0 / np.sqrt(T)


def setup_inputs():
    u = mx_kscale(T)
    return {"q_rot": bf(np.random.standard_normal((B, H, T, D)) * QS * u[:, None]),
            "v": bf(np.random.standard_normal((B, H, T, D)) * VS / (u * u.max())[:, None])}


def reference(q_rot, v):
    scores = f64(q_rot) @ f64(q_rot).transpose(0, 1, 3, 2)
    return mxq(scores, 3, "e4m3") @ mxq(f64(v), 2, "e4m3")

@@ -1,0 +1,219 @@
+from contextlib import ExitStack
+
+import concourse.mybir as mybir
+from concourse.masks import make_identity
+
+F32 = mybir.dt.float32
+BF16 = mybir.dt.bfloat16
+U32 = mybir.dt.uint32
+U8 = mybir.dt.uint8
+FP8X4 = mybir.dt.float8_e4m3fn_x4
+
+NB = 8
+T = 512
+D = 1024
+P = 128
+NT = T // P
+ND = D // P
+HALF = 512
+FLOPS = 2 * NB * T * T * D * 2
+
+RING = 4
+
+
+def tile_linearattention_pa_t_kernel(tc, q_rot, v, out):
+    nc = tc.nc
+    qv = q_rot.rearrange("b h (p j) d -> (b h) p j d", j=NT)
+    vv = v.rearrange("b h (p j) d -> (b h) p j d", j=NT)
+    ov = out.rearrange("b h (p j) d -> (b h) p j d", j=NT)
+
+    with ExitStack() as ctx:
+        ctx.enter_context(tc.manual_schedule())
+        const = ctx.enter_context(tc.tile_pool(name="const", bufs=1))
+        qpool = ctx.enter_context(tc.tile_pool(name="qpool", bufs=RING))
+        vpool = ctx.enter_context(tc.tile_pool(name="vpool", bufs=RING))
+        qtpool = ctx.enter_context(tc.tile_pool(name="qtpool", bufs=2))
+        vgpool = ctx.enter_context(tc.tile_pool(name="vgpool", bufs=1))
+        mxpool = ctx.enter_context(tc.tile_pool(name="mxpool", bufs=2))
+        upool = ctx.enter_context(tc.tile_pool(name="upool", bufs=2))
+        opool = ctx.enter_context(tc.tile_pool(name="opool", bufs=3))
+        psum = ctx.enter_context(tc.psum_pool(name="psum", bufs=1))
+
+        ident_bf = const.tile([P, P], BF16, name="ident_bf", tag="ident_bf")
+        make_identity(nc, ident_bf[:])
+        ident_f = const.tile([P, P], F32, name="ident_f", tag="ident_f")
+        make_identity(nc, ident_f[:])
+
+        q_sb = {}
+        v_sb = {}
+        q_t = {}
+        s_ps = {}
+        u_sb = {}
+        s_grp = {}
+        s_cod = {}
+        s_scl = {}
+        v_grp = {}
+        v_cod = {}
+        v_scl = {}
+        o_sb = {}
+
+        def load_q(i, parts):
+            q_sb[i] = qpool.tile([P, NT, D], BF16, name="q_sb", tag="q_sb")
+            if parts:
+                for j in range(NT):
+                    nc.sync.dma_start(out=q_sb[i][:, j, :], in_=qv[i][:, j, :])
+            else:
+                nc.sync.dma_start(out=q_sb[i][:], in_=qv[i])
+
+        def load_v(i):
+            v_sb[i] = vpool.tile([P, NT, D], BF16, name="v_sb", tag="v_sb")
+            nc.sync.dma_start(out=v_sb[i][:], in_=vv[i])
+
+        def transpose_q(i):
+            q_t[i] = qtpool.tile([P, ND, T], BF16, name="q_t", tag="q_t")
+            for j in range(NT):
+                bank = psum.tile([P, ND, P], BF16, name="qt_ps", tag="P%d" % j)
+                for k in range(ND):
+                    nc.tensor.transpose(bank[:, k, :], q_sb[i][:, j, k * P:(k + 1) * P], ident_bf[:])
+                dst = q_t[i][:, :, j * P:(j + 1) * P]
+                if j % 2 == 0:
+                    nc.scalar.copy(out=dst, in_=bank[:])
+                else:
+                    nc.vector.tensor_copy(out=dst, in_=bank[:])
+
+        def scores(i, b):
+            s_ps[i, b] = psum.tile([P, NT, P], F32, name="s_ps", tag="S%d" % b)
+            for j in range(b + 1):
+                for k in range(ND):
+                    nc.tensor.matmul(
+                        s_ps[i, b][:, j, :],
+                        lhsT=q_t[i][:, k, j * P:(j + 1) * P],
+                        rhs=q_t[i][:, k, b * P:(b + 1) * P],
+                        start=(k == 0),
+                        stop=(k == ND - 1),
+                    )
+
+        def upper_out(i, b):
+            u_sb[i, b] = upool.tile([P, b, P], F32, name="u_sb%d" % b, tag="u_sb%d" % b)
+            nc.vector.tensor_copy(out=u_sb[i, b][:], in_=s_ps[i, b][:, 0:b, :])
+
+        def mirror(i):
+            for tgt in (2, 1, 0):
+                for src in range(NT - 1, tgt, -1):
+                    nc.tensor.transpose(s_ps[i, tgt][:, src, :], u_sb[i, src][:, tgt, :], ident_f[:])
+
+        def group_s(i, b):
+            if b == NT - 1:
+                s_grp[i] = mxpool.tile([P, NT, P, NT], BF16, name="s_grp", tag="s_grp", align_bytes=64)
+                s_cod[i] = mxpool.tile([P, T], U32, name="s_cod", tag="s_cod", align_bytes=64)
+                s_scl[i] = mxpool.tile([P, T], U8, name="s_scl", tag="s_scl", align_bytes=64)
+            nc.vector.tensor_copy(out=s_grp[i][:, b], in_=s_ps[i, b][:].rearrange("p j m -> p m j"))
+
+        def quant_s(i, b):
+            cols = slice(b * P, (b + 1) * P)
+            nc.vector.quantize_mx(
+                out=s_cod[i][:, cols].bitcast(FP8X4),
+                scales=s_scl[i][:, cols],
+                in_=s_grp[i][:, b].rearrange("p m j -> p (m j)"),
+            )
+
+        def group_v(i, h):
+            if h == 0:
+                v_grp[i] = vgpool.tile([P, D, NT], BF16, name="v_grp", tag="v_grp", align_bytes=64)
+            cols = slice(h * HALF, (h + 1) * HALF)
+            nc.vector.tensor_copy(
+                out=v_grp[i][:, cols, :].rearrange("p (c r) j -> p c j r", r=4),
+                in_=v_sb[i][:, :, cols].rearrange("p j (c r) -> p c j r", r=4),
+            )
+
+        def quant_v(i):
+            v_cod[i] = mxpool.tile([P, D], U32, name="v_cod", tag="v_cod", align_bytes=64)
+            v_scl[i] = mxpool.tile([P, D], U8, name="v_scl", tag="v_scl", align_bytes=64)
+            nc.vector.quantize_mx(
+                out=v_cod[i][:].bitcast(FP8X4),
+                scales=v_scl[i][:],
+                in_=v_grp[i][:].rearrange("p c j -> p (c j)"),
+            )
+
+        def second(i, b, both):
+            if b == NT - 1:
+                o_sb[i] = opool.tile([P, NT, D], F32, name="o_sb", tag="o_sb")
+            rows = slice(b * P, (b + 1) * P)
+            first_bank = 0 if b % 2 == 1 else 2
+            for h in range(2):
+                cols = slice(h * HALF, (h + 1) * HALF)
+                acc = psum.tile([P, HALF], F32, name="o_ps", tag="P%d" % (first_bank + h))
+                nc.tensor.matmul_mx(
+                    out=acc[:],
+                    lhsT=s_cod[i][:, rows].bitcast(FP8X4),
+                    lhsT_scale=s_scl[i][:, rows],
+                    rhs=v_cod[i][:, cols].bitcast(FP8X4),
+                    rhs_scale=v_scl[i][:, cols],
+                    start=True,
+                    stop=True,
+                )
+                if both and h == 1:
+                    nc.vector.tensor_copy(out=o_sb[i][:, b, cols], in_=acc[:])
+                else:
+                    nc.scalar.copy(out=o_sb[i][:, b, cols], in_=acc[:])
+
+        def store(i, lo, hi):
+            nc.sync.dma_start(out=ov[i][:, lo:hi, :], in_=o_sb[i][:, lo:hi, :])
+
+        load_q(0, True)
+        load_v(0)
+        for i in range(1, RING):
+            load_q(i, False)
+            load_v(i)
+        transpose_q(0)
+        group_v(0, 0)
+        group_v(0, 1)
+        quant_v(0)
+
+        for i in range(NB):
+            prev = i - 1
+            nxt = i + 1
+            if i + RING < NB:
+                load_q(i + RING, False)
+                load_v(i + RING)
+            if prev >= 0:
+                group_s(prev, 2)
+                group_s(prev, 1)
+                quant_s(prev, 2)
+                group_s(prev, 0)
+                quant_s(prev, 1)
+                quant_s(prev, 0)
+            scores(i, 3)
+            upper_out(i, 3)
+            group_s(i, 3)
+            if prev >= 0:
+                second(prev, 2, False)
+                store(prev, 2, 4)
+            scores(i, 2)
+            if nxt < NB:
+                group_v(nxt, 0)
+            quant_s(i, 3)
+            upper_out(i, 2)
+            if prev >= 0:
+                second(prev, 1, False)
+            scores(i, 1)
+            if nxt < NB:
+                group_v(nxt, 1)
+            upper_out(i, 1)
+            if prev >= 0:
+                second(prev, 0, False)
+                store(prev, 0, 2)
+            scores(i, 0)
+            if nxt < NB:
+                quant_v(nxt)
+                transpose_q(nxt)
+            mirror(i)
+            second(i, 3, False)
+
+        last = NB - 1
+        store(last, 3, 4)
+        for b in (2, 1, 0):
+            group_s(last, b)
+            quant_s(last, b)
+            second(last, b, True)
+            store(last, b, b + 1)

@@ -17,13 +17,13 @@ NT = T // P
 ND = D // P
 HALF = 512
 FLOPS = 2 * NB * T * T * D * 2
-
 RING = 4
+WORDS = False
 
 
 def tile_linearattention_pa_t_kernel(tc, q_rot, v, out):
     nc = tc.nc
-    qv = q_rot.rearrange("b h (p j) d -> (b h) p j d", j=NT)
+    qv = q_rot.rearrange("b h (p j) d -> (b h) p (j d)", j=NT)
     vv = v.rearrange("b h (p j) d -> (b h) p j d", j=NT)
     ov = out.rearrange("b h (p j) d -> (b h) p j d", j=NT)
 
@@ -39,10 +39,11 @@ def tile_linearattention_pa_t_kernel(tc, q_rot, v, out):
         opool = ctx.enter_context(tc.tile_pool(name="opool", bufs=3))
         psum = ctx.enter_context(tc.psum_pool(name="psum", bufs=1))
 
-        ident_bf = const.tile([P, P], BF16, name="ident_bf", tag="ident_bf")
-        make_identity(nc, ident_bf[:])
         ident_f = const.tile([P, P], F32, name="ident_f", tag="ident_f")
         make_identity(nc, ident_f[:])
+        if not WORDS:
+            ident_bf = const.tile([P, P], BF16, name="ident_bf", tag="ident_bf")
+            make_identity(nc, ident_bf[:])
 
         q_sb = {}
         v_sb = {}
@@ -57,11 +58,17 @@ def tile_linearattention_pa_t_kernel(tc, q_rot, v, out):
         v_scl = {}
         o_sb = {}
 
+        def copy_on(eng, dst, src):
+            if eng == "act":
+                nc.scalar.copy(out=dst, in_=src)
+            else:
+                nc.vector.tensor_copy(out=dst, in_=src)
+
         def load_q(i, parts):
-            q_sb[i] = qpool.tile([P, NT, D], BF16, name="q_sb", tag="q_sb")
+            q_sb[i] = qpool.tile([P, NT * D], BF16, name="q_sb", tag="q_sb")
             if parts:
                 for j in range(NT):
-                    nc.sync.dma_start(out=q_sb[i][:, j, :], in_=qv[i][:, j, :])
+                    nc.sync.dma_start(out=q_sb[i][:, j * D:(j + 1) * D], in_=qv[i][:, j * D:(j + 1) * D])
             else:
                 nc.sync.dma_start(out=q_sb[i][:], in_=qv[i])
 
@@ -70,16 +77,31 @@ def tile_linearattention_pa_t_kernel(tc, q_rot, v, out):
             nc.sync.dma_start(out=v_sb[i][:], in_=vv[i])
 
         def transpose_q(i):
-            q_t[i] = qtpool.tile([P, ND, T], BF16, name="q_t", tag="q_t")
-            for j in range(NT):
-                bank = psum.tile([P, ND, P], BF16, name="qt_ps", tag="P%d" % j)
-                for k in range(ND):
-                    nc.tensor.transpose(bank[:, k, :], q_sb[i][:, j, k * P:(k + 1) * P], ident_bf[:])
-                dst = q_t[i][:, :, j * P:(j + 1) * P]
-                if j % 2 == 0:
-                    nc.scalar.copy(out=dst, in_=bank[:])
-                else:
-                    nc.vector.tensor_copy(out=dst, in_=bank[:])
+            if WORDS:
+                q_t[i] = qtpool.tile([P, (ND // 2) * T], F32, name="q_t", tag="q_t")
+                words = q_sb[i][:].bitcast(F32)
+                dst_all = q_t[i][:].rearrange("p (c m) -> p c m", c=ND // 2)
+                for j in range(NT):
+                    bank = psum.tile([P, ND // 2, P], F32, name="qt_ps", tag="P%d" % j)
+                    for c in range(ND // 2):
+                        lo = j * (D // 2) + c * P
+                        nc.tensor.transpose(bank[:, c, :], words[:, lo:lo + P], ident_f[:])
+                    copy_on("act" if j % 2 == 0 else "dve", dst_all[:, :, j * P:(j + 1) * P], bank[:])
+            else:
+                q_t[i] = qtpool.tile([P, ND * T], BF16, name="q_t", tag="q_t")
+                dst_all = q_t[i][:].rearrange("p (k m) -> p k m", k=ND)
+                for j in range(NT):
+                    bank = psum.tile([P, ND, P], BF16, name="qt_ps", tag="P%d" % j)
+                    for k in range(ND):
+                        lo = j * D + k * P
+                        nc.tensor.transpose(bank[:, k, :], q_sb[i][:, lo:lo + P], ident_bf[:])
+                    copy_on("act" if j % 2 == 0 else "dve", dst_all[:, :, j * P:(j + 1) * P], bank[:])
+
+        def q_cols(i, k, j):
+            if WORDS:
+                view = q_t[i][:].bitcast(BF16).rearrange("p (c m e) -> p c m e", c=ND // 2, e=2)
+                return view[:, k // 2, j * P:(j + 1) * P, k % 2]
+            return q_t[i][:, k * T + j * P:k * T + (j + 1) * P]
 
         def scores(i, b):
             s_ps[i, b] = psum.tile([P, NT, P], F32, name="s_ps", tag="S%d" % b)
@@ -87,27 +109,26 @@ def tile_linearattention_pa_t_kernel(tc, q_rot, v, out):
                 for k in range(ND):
                     nc.tensor.matmul(
                         s_ps[i, b][:, j, :],
-                        lhsT=q_t[i][:, k, j * P:(j + 1) * P],
-                        rhs=q_t[i][:, k, b * P:(b + 1) * P],
+                        lhsT=q_cols(i, k, j),
+                        rhs=q_cols(i, k, b),
                         start=(k == 0),
                         stop=(k == ND - 1),
                     )
 
-        def upper_out(i, b):
+        def upper_out(i, b, eng):
             u_sb[i, b] = upool.tile([P, b, P], F32, name="u_sb%d" % b, tag="u_sb%d" % b)
-            nc.vector.tensor_copy(out=u_sb[i, b][:], in_=s_ps[i, b][:, 0:b, :])
+            copy_on(eng, u_sb[i, b][:], s_ps[i, b][:, 0:b, :])
 
-        def mirror(i):
-            for tgt in (2, 1, 0):
-                for src in range(NT - 1, tgt, -1):
-                    nc.tensor.transpose(s_ps[i, tgt][:, src, :], u_sb[i, src][:, tgt, :], ident_f[:])
+        def mirror(i, tgt):
+            for src in range(NT - 1, tgt, -1):
+                nc.tensor.transpose(s_ps[i, tgt][:, src, :], u_sb[i, src][:, tgt, :], ident_f[:])
 
-        def group_s(i, b):
+        def group_s(i, b, eng):
             if b == NT - 1:
                 s_grp[i] = mxpool.tile([P, NT, P, NT], BF16, name="s_grp", tag="s_grp", align_bytes=64)
                 s_cod[i] = mxpool.tile([P, T], U32, name="s_cod", tag="s_cod", align_bytes=64)
                 s_scl[i] = mxpool.tile([P, T], U8, name="s_scl", tag="s_scl", align_bytes=64)
-            nc.vector.tensor_copy(out=s_grp[i][:, b], in_=s_ps[i, b][:].rearrange("p j m -> p m j"))
+            copy_on(eng, s_grp[i][:, b], s_ps[i, b][:].rearrange("p j m -> p m j"))
 
         def quant_s(i, b):
             cols = slice(b * P, (b + 1) * P)
@@ -135,14 +156,14 @@ def tile_linearattention_pa_t_kernel(tc, q_rot, v, out):
                 in_=v_grp[i][:].rearrange("p c j -> p (c j)"),
             )
 
-        def second(i, b, both):
+        def second(i, b, tags, engs):
             if b == NT - 1:
                 o_sb[i] = opool.tile([P, NT, D], F32, name="o_sb", tag="o_sb")
             rows = slice(b * P, (b + 1) * P)
-            first_bank = 0 if b % 2 == 1 else 2
+            accs = []
             for h in range(2):
                 cols = slice(h * HALF, (h + 1) * HALF)
-                acc = psum.tile([P, HALF], F32, name="o_ps", tag="P%d" % (first_bank + h))
+                acc = psum.tile([P, HALF], F32, name="o_ps", tag=tags[h])
                 nc.tensor.matmul_mx(
                     out=acc[:],
                     lhsT=s_cod[i][:, rows].bitcast(FP8X4),
@@ -152,68 +173,88 @@ def tile_linearattention_pa_t_kernel(tc, q_rot, v, out):
                     start=True,
                     stop=True,
                 )
-                if both and h == 1:
-                    nc.vector.tensor_copy(out=o_sb[i][:, b, cols], in_=acc[:])
-                else:
-                    nc.scalar.copy(out=o_sb[i][:, b, cols], in_=acc[:])
+                accs.append(acc)
+            for h in range(2):
+                cols = slice(h * HALF, (h + 1) * HALF)
+                copy_on(engs[h], o_sb[i][:, b, cols], accs[h][:])
 
         def store(i, lo, hi):
             nc.sync.dma_start(out=ov[i][:, lo:hi, :], in_=o_sb[i][:, lo:hi, :])
 
+        AA = ("act", "act")
         load_q(0, True)
         load_v(0)
         for i in range(1, RING):
             load_q(i, False)
             load_v(i)
         transpose_q(0)
-        group_v(0, 0)
-        group_v(0, 1)
-        quant_v(0)
 
         for i in range(NB):
             prev = i - 1
             nxt = i + 1
+            final = i == NB - 1
             if i + RING < NB:
                 load_q(i + RING, False)
-                load_v(i + RING)
+            if prev >= 0 and prev + RING < NB:
+                load_v(prev + RING)
             if prev >= 0:
-                group_s(prev, 2)
-                group_s(prev, 1)
+                group_s(prev, 2, "dve")
+                group_s(prev, 1, "dve")
                 quant_s(prev, 2)
-                group_s(prev, 0)
+                group_s(prev, 0, "dve")
                 quant_s(prev, 1)
                 quant_s(prev, 0)
+            if i == 0:
+                scores(i, 1)
+                upper_out(i, 1, "act")
             scores(i, 3)
-            upper_out(i, 3)
-            group_s(i, 3)
+            upper_out(i, 3, "act")
+            group_s(i, 3, "act")
             if prev >= 0:
-                second(prev, 2, False)
+                second(prev, 3, ("P0", "P1"), AA)
+                second(prev, 2, ("P2", "P3"), AA)
                 store(prev, 2, 4)
-            scores(i, 2)
-            if nxt < NB:
-                group_v(nxt, 0)
+            group_v(i, 0)
             quant_s(i, 3)
-            upper_out(i, 2)
-            if prev >= 0:
-                second(prev, 1, False)
-            scores(i, 1)
-            if nxt < NB:
-                group_v(nxt, 1)
-            upper_out(i, 1)
-            if prev >= 0:
-                second(prev, 0, False)
+            group_v(i, 1)
+            scores(i, 2)
+            upper_out(i, 2, "dve" if final else "act")
+            if final:
+                quant_v(i)
+                second(prev, 1, ("P0", "P1"), AA)
+                second(prev, 0, ("P2", "P3"), AA)
                 store(prev, 0, 2)
-            scores(i, 0)
-            if nxt < NB:
-                quant_v(nxt)
+                mirror(i, 2)
+                group_s(i, 2, "dve")
+                quant_s(i, 2)
+                scores(i, 1)
+                upper_out(i, 1, "dve")
+                second(i, 3, ("S3", "P0"), AA)
+                store(i, 3, 4)
+                mirror(i, 1)
+                group_s(i, 1, "dve")
+                quant_s(i, 1)
+                scores(i, 0)
+                mirror(i, 0)
+                group_s(i, 0, "dve")
+                quant_s(i, 0)
+                second(i, 2, ("P1", "P2"), AA)
+                store(i, 2, 3)
+                second(i, 1, ("P3", "S3"), AA)
+                store(i, 1, 2)
+                second(i, 0, ("S2", "S1"), ("act", "dve"))
+                store(i, 0, 1)
+            else:
                 transpose_q(nxt)
-            mirror(i)
-            second(i, 3, False)
-
-        last = NB - 1
-        store(last, 3, 4)
-        for b in (2, 1, 0):
-            group_s(last, b)
-            quant_s(last, b)
-            second(last, b, True)
-            store(last, b, b + 1)
+                if i > 0:
+                    scores(i, 1)
+                    upper_out(i, 1, "act")
+                if prev >= 0:
+                    second(prev, 1, ("P0", "P1"), AA)
+                    second(prev, 0, ("P2", "P3"), AA)
+                    store(prev, 0, 2)
+                quant_v(i)
+                scores(i, 0)
+                mirror(i, 2)
+                mirror(i, 1)
+                mirror(i, 0)

@@ -18,7 +18,7 @@ ND = D // P
 HALF = 512
 FLOPS = 2 * NB * T * T * D * 2
 RING = 4
-WORDS = False
+WORDS = True
 
 
 def tile_linearattention_pa_t_kernel(tc, q_rot, v, out):

@@ -19,6 +19,7 @@ HALF = 512
 FLOPS = 2 * NB * T * T * D * 2
 RING = 4
 WORDS = True
+QT_TAGS = ("P2", "P3", "P0", "P1")
 
 
 def tile_linearattention_pa_t_kernel(tc, q_rot, v, out):
@@ -82,7 +83,7 @@ def tile_linearattention_pa_t_kernel(tc, q_rot, v, out):
                 words = q_sb[i][:].bitcast(F32)
                 dst_all = q_t[i][:].rearrange("p (c m) -> p c m", c=ND // 2)
                 for j in range(NT):
-                    bank = psum.tile([P, ND // 2, P], F32, name="qt_ps", tag="P%d" % j)
+                    bank = psum.tile([P, ND // 2, P], F32, name="qt_ps", tag=QT_TAGS[j])
                     for c in range(ND // 2):
                         lo = j * (D // 2) + c * P
                         nc.tensor.transpose(bank[:, c, :], words[:, lo:lo + P], ident_f[:])
@@ -91,7 +92,7 @@ def tile_linearattention_pa_t_kernel(tc, q_rot, v, out):
                 q_t[i] = qtpool.tile([P, ND * T], BF16, name="q_t", tag="q_t")
                 dst_all = q_t[i][:].rearrange("p (k m) -> p k m", k=ND)
                 for j in range(NT):
-                    bank = psum.tile([P, ND, P], BF16, name="qt_ps", tag="P%d" % j)
+                    bank = psum.tile([P, ND, P], BF16, name="qt_ps", tag=QT_TAGS[j])
                     for k in range(ND):
                         lo = j * D + k * P
                         nc.tensor.transpose(bank[:, k, :], q_sb[i][:, lo:lo + P], ident_bf[:])
@@ -212,11 +213,11 @@ def tile_linearattention_pa_t_kernel(tc, q_rot, v, out):
             group_s(i, 3, "act")
             if prev >= 0:
                 second(prev, 3, ("P0", "P1"), AA)
-                second(prev, 2, ("P2", "P3"), AA)
+                second(prev, 2, ("S1", "S0"), AA)
                 store(prev, 2, 4)
             group_v(i, 0)
-            quant_s(i, 3)
             group_v(i, 1)
+            quant_s(i, 3)
             scores(i, 2)
             upper_out(i, 2, "dve" if final else "act")
             if final:
@@ -250,8 +251,8 @@ def tile_linearattention_pa_t_kernel(tc, q_rot, v, out):
                     scores(i, 1)
                     upper_out(i, 1, "act")
                 if prev >= 0:
-                    second(prev, 1, ("P0", "P1"), AA)
-                    second(prev, 0, ("P2", "P3"), AA)
+                    second(prev, 1, ("S3", "P2"), AA)
+                    second(prev, 0, ("P3", "P0"), AA)
                     store(prev, 0, 2)
                 quant_v(i)
                 scores(i, 0)

@@ -7,6 +7,7 @@ F32 = mybir.dt.float32
 BF16 = mybir.dt.bfloat16
 U32 = mybir.dt.uint32
 U8 = mybir.dt.uint8
+I32 = mybir.dt.int32
 FP8X4 = mybir.dt.float8_e4m3fn_x4
 
 NB = 8
@@ -19,6 +20,8 @@ HALF = 512
 FLOPS = 2 * NB * T * T * D * 2
 RING = 4
 WORDS = True
+WARM_N = 256
+WARM_FIRST = 7
 QT_TAGS = ("P2", "P3", "P0", "P1")
 
 
@@ -45,6 +48,14 @@ def tile_linearattention_pa_t_kernel(tc, q_rot, v, out):
         if not WORDS:
             ident_bf = const.tile([P, P], BF16, name="ident_bf", tag="ident_bf")
             make_identity(nc, ident_bf[:])
+
+        warm = const.tile([P, HALF], BF16, name="warm", tag="warm")
+        nc.vector.memset(warm[:].bitcast(I32), 0)
+        warm_ps = psum.tile([P, HALF], F32, name="warm_ps", tag="S0")
+
+        def idle_pass(n):
+            for r in range(n):
+                nc.tensor.matmul(warm_ps[:, 0:WARM_N], lhsT=warm[:, 0:P], rhs=warm[:, 0:WARM_N], start=True, stop=True)
 
         q_sb = {}
         v_sb = {}
@@ -77,7 +88,7 @@ def tile_linearattention_pa_t_kernel(tc, q_rot, v, out):
             v_sb[i] = vpool.tile([P, NT, D], BF16, name="v_sb", tag="v_sb")
             nc.sync.dma_start(out=v_sb[i][:], in_=vv[i])
 
-        def transpose_q(i):
+        def transpose_q(i, fill=0):
             if WORDS:
                 q_t[i] = qtpool.tile([P, (ND // 2) * T], F32, name="q_t", tag="q_t")
                 words = q_sb[i][:].bitcast(F32)
@@ -87,6 +98,8 @@ def tile_linearattention_pa_t_kernel(tc, q_rot, v, out):
                     for c in range(ND // 2):
                         lo = j * (D // 2) + c * P
                         nc.tensor.transpose(bank[:, c, :], words[:, lo:lo + P], ident_f[:])
+                    if j < NT - 1:
+                        idle_pass(fill)
                     copy_on("act" if j % 2 == 0 else "dve", dst_all[:, :, j * P:(j + 1) * P], bank[:])
             else:
                 q_t[i] = qtpool.tile([P, ND * T], BF16, name="q_t", tag="q_t")
@@ -139,18 +152,20 @@ def tile_linearattention_pa_t_kernel(tc, q_rot, v, out):
                 in_=s_grp[i][:, b].rearrange("p m j -> p (m j)"),
             )
 
-        def group_v(i, h):
+        def group_v(i, h, eng="dve"):
             if h == 0:
-                v_grp[i] = vgpool.tile([P, D, NT], BF16, name="v_grp", tag="v_grp", align_bytes=64)
+                tag = "v_grp" if eng == "dve" else "v_grp_act"
+                v_grp[i] = vgpool.tile([P, D, NT], BF16, name=tag, tag=tag, align_bytes=64)
             cols = slice(h * HALF, (h + 1) * HALF)
-            nc.vector.tensor_copy(
-                out=v_grp[i][:, cols, :].rearrange("p (c r) j -> p c j r", r=4),
-                in_=v_sb[i][:, :, cols].rearrange("p j (c r) -> p c j r", r=4),
+            copy_on(
+                eng,
+                v_grp[i][:, cols, :].rearrange("p (c r) j -> p c j r", r=4),
+                v_sb[i][:, :, cols].rearrange("p j (c r) -> p c j r", r=4),
             )
 
         def quant_v(i):
-            v_cod[i] = mxpool.tile([P, D], U32, name="v_cod", tag="v_cod", align_bytes=64)
-            v_scl[i] = mxpool.tile([P, D], U8, name="v_scl", tag="v_scl", align_bytes=64)
+            v_cod[i] = mxpool.tile([P, D], U32, name="v_cod", tag="v_cod", align_bytes=64, bufs=3)
+            v_scl[i] = mxpool.tile([P, D], U8, name="v_scl", tag="v_scl", align_bytes=64, bufs=3)
             nc.vector.quantize_mx(
                 out=v_cod[i][:].bitcast(FP8X4),
                 scales=v_scl[i][:],
@@ -179,6 +194,14 @@ def tile_linearattention_pa_t_kernel(tc, q_rot, v, out):
                 cols = slice(h * HALF, (h + 1) * HALF)
                 copy_on(engs[h], o_sb[i][:, b, cols], accs[h][:])
 
+        def finish_scores(i):
+            group_s(i, 2, "dve")
+            group_s(i, 1, "dve")
+            quant_s(i, 2)
+            group_s(i, 0, "dve")
+            quant_s(i, 1)
+            quant_s(i, 0)
+
         def store(i, lo, hi):
             nc.sync.dma_start(out=ov[i][:, lo:hi, :], in_=o_sb[i][:, lo:hi, :])
 
@@ -188,23 +211,20 @@ def tile_linearattention_pa_t_kernel(tc, q_rot, v, out):
         for i in range(1, RING):
             load_q(i, False)
             load_v(i)
-        transpose_q(0)
+        idle_pass(WARM_FIRST)
+        transpose_q(0, 2)
 
-        for i in range(NB):
+        for i in range(NB - 1):
             prev = i - 1
             nxt = i + 1
-            final = i == NB - 1
             if i + RING < NB:
                 load_q(i + RING, False)
             if prev >= 0 and prev + RING < NB:
                 load_v(prev + RING)
+            if i >= NB - 3:
+                group_v(NB - 1, i - (NB - 3), "act")
             if prev >= 0:
-                group_s(prev, 2, "dve")
-                group_s(prev, 1, "dve")
-                quant_s(prev, 2)
-                group_s(prev, 0, "dve")
-                quant_s(prev, 1)
-                quant_s(prev, 0)
+                finish_scores(prev)
             if i == 0:
                 scores(i, 1)
                 upper_out(i, 1, "act")
@@ -219,43 +239,55 @@ def tile_linearattention_pa_t_kernel(tc, q_rot, v, out):
             group_v(i, 1)
             quant_s(i, 3)
             scores(i, 2)
-            upper_out(i, 2, "dve" if final else "act")
-            if final:
-                quant_v(i)
-                second(prev, 1, ("P0", "P1"), AA)
-                second(prev, 0, ("P2", "P3"), AA)
-                store(prev, 0, 2)
-                mirror(i, 2)
-                group_s(i, 2, "dve")
-                quant_s(i, 2)
+            upper_out(i, 2, "act")
+            transpose_q(nxt)
+            if i > 0:
                 scores(i, 1)
-                upper_out(i, 1, "dve")
-                second(i, 3, ("S3", "P0"), AA)
-                store(i, 3, 4)
-                mirror(i, 1)
-                group_s(i, 1, "dve")
-                quant_s(i, 1)
-                scores(i, 0)
-                mirror(i, 0)
-                group_s(i, 0, "dve")
-                quant_s(i, 0)
-                second(i, 2, ("P1", "P2"), AA)
-                store(i, 2, 3)
-                second(i, 1, ("P3", "S3"), AA)
-                store(i, 1, 2)
-                second(i, 0, ("S2", "S1"), ("act", "dve"))
-                store(i, 0, 1)
-            else:
-                transpose_q(nxt)
-                if i > 0:
-                    scores(i, 1)
-                    upper_out(i, 1, "act")
-                if prev >= 0:
-                    second(prev, 1, ("S3", "P2"), AA)
-                    second(prev, 0, ("P3", "P0"), AA)
-                    store(prev, 0, 2)
-                quant_v(i)
-                scores(i, 0)
-                mirror(i, 2)
-                mirror(i, 1)
-                mirror(i, 0)
+                upper_out(i, 1, "act")
+            if prev >= 0:
+                second(prev, 1, ("S3", "P2"), AA)
+                second(prev, 0, ("P3", "P0"), AA)
+                store(prev, 0, 2)
+            quant_v(i)
+            if i == NB - 2:
+                quant_v(NB - 1)
+            scores(i, 0)
+            mirror(i, 2)
+            mirror(i, 1)
+            mirror(i, 0)
+
+        i = NB - 1
+        prev = i - 1
+        finish_scores(prev)
+        scores(i, 3)
+        second(prev, 3, ("P0", "P1"), AA)
+        second(prev, 2, ("S1", "S0"), ("dve", "dve"))
+        store(prev, 2, 4)
+        upper_out(i, 3, "act")
+        group_s(i, 3, "act")
+        scores(i, 2)
+        upper_out(i, 2, "dve")
+        quant_s(i, 3)
+        second(prev, 1, ("P2", "P3"), AA)
+        second(prev, 0, ("P0", "P1"), ("dve", "act"))
+        store(prev, 0, 2)
+        mirror(i, 2)
+        group_s(i, 2, "dve")
+        quant_s(i, 2)
+        scores(i, 1)
+        upper_out(i, 1, "dve")
+        second(i, 3, ("S3", "P2"), AA)
+        store(i, 3, 4)
+        mirror(i, 1)
+        group_s(i, 1, "dve")
+        quant_s(i, 1)
+        second(i, 2, ("P3", "P0"), AA)
+        store(i, 2, 3)
+        scores(i, 0)
+        mirror(i, 0)
+        group_s(i, 0, "dve")
+        quant_s(i, 0)
+        second(i, 1, ("P1", "S3"), AA)
+        store(i, 1, 2)
+        second(i, 0, ("S2", "S1"), ("act", "dve"))
+        store(i, 0, 1)

@@ -16,13 +16,18 @@ D = 1024
 P = 128
 NT = T // P
 ND = D // P
+NW = ND // 2
 HALF = 512
 FLOPS = 2 * NB * T * T * D * 2
 RING = 4
-WORDS = True
 WARM_N = 256
 WARM_FIRST = 7
-QT_TAGS = ("P2", "P3", "P0", "P1")
+J_ORDER = (3, 0, 1, 2)
+GROUPS = tuple((b, j) for b in (3, 2, 1, 0) for j in range(b + 1))
+LAST_GROUPS = GROUPS[0:8] + ((0, 0), (1, 1))
+N_MM = len(GROUPS) * ND
+N_SLOTS = 22
+SLOT_AT = tuple((n + 1) * N_MM // N_SLOTS for n in range(N_SLOTS))
 
 
 def tile_linearattention_pa_t_kernel(tc, q_rot, v, out):
@@ -45,9 +50,6 @@ def tile_linearattention_pa_t_kernel(tc, q_rot, v, out):
 
         ident_f = const.tile([P, P], F32, name="ident_f", tag="ident_f")
         make_identity(nc, ident_f[:])
-        if not WORDS:
-            ident_bf = const.tile([P, P], BF16, name="ident_bf", tag="ident_bf")
-            make_identity(nc, ident_bf[:])
 
         warm = const.tile([P, HALF], BF16, name="warm", tag="warm")
         nc.vector.memset(warm[:].bitcast(I32), 0)
@@ -59,6 +61,7 @@ def tile_linearattention_pa_t_kernel(tc, q_rot, v, out):
 
         q_sb = {}
         v_sb = {}
+        qt_ps = {}
         q_t = {}
         s_ps = {}
         u_sb = {}
@@ -79,7 +82,7 @@ def tile_linearattention_pa_t_kernel(tc, q_rot, v, out):
         def load_q(i, parts):
             q_sb[i] = qpool.tile([P, NT * D], BF16, name="q_sb", tag="q_sb")
             if parts:
-                for j in range(NT):
+                for j in J_ORDER:
                     nc.sync.dma_start(out=q_sb[i][:, j * D:(j + 1) * D], in_=qv[i][:, j * D:(j + 1) * D])
             else:
                 nc.sync.dma_start(out=q_sb[i][:], in_=qv[i])
@@ -88,54 +91,40 @@ def tile_linearattention_pa_t_kernel(tc, q_rot, v, out):
             v_sb[i] = vpool.tile([P, NT, D], BF16, name="v_sb", tag="v_sb")
             nc.sync.dma_start(out=v_sb[i][:], in_=vv[i])
 
-        def transpose_q(i, fill=0):
-            if WORDS:
-                q_t[i] = qtpool.tile([P, (ND // 2) * T], F32, name="q_t", tag="q_t")
-                words = q_sb[i][:].bitcast(F32)
-                dst_all = q_t[i][:].rearrange("p (c m) -> p c m", c=ND // 2)
-                for j in range(NT):
-                    bank = psum.tile([P, ND // 2, P], F32, name="qt_ps", tag=QT_TAGS[j])
-                    for c in range(ND // 2):
-                        lo = j * (D // 2) + c * P
-                        nc.tensor.transpose(bank[:, c, :], words[:, lo:lo + P], ident_f[:])
-                    if j < NT - 1:
-                        idle_pass(fill)
-                    copy_on("act" if j % 2 == 0 else "dve", dst_all[:, :, j * P:(j + 1) * P], bank[:])
-            else:
-                q_t[i] = qtpool.tile([P, ND * T], BF16, name="q_t", tag="q_t")
-                dst_all = q_t[i][:].rearrange("p (k m) -> p k m", k=ND)
-                for j in range(NT):
-                    bank = psum.tile([P, ND, P], BF16, name="qt_ps", tag=QT_TAGS[j])
-                    for k in range(ND):
-                        lo = j * D + k * P
-                        nc.tensor.transpose(bank[:, k, :], q_sb[i][:, lo:lo + P], ident_bf[:])
-                    copy_on("act" if j % 2 == 0 else "dve", dst_all[:, :, j * P:(j + 1) * P], bank[:])
+        def turn_q(i, j, c, tag):
+            if c == 0:
+                qt_ps[i, j] = psum.tile([P, NW * P], F32, name="qt_ps", tag=tag)
+            lo = j * (D // 2) + c * P
+            nc.tensor.transpose(qt_ps[i, j][:, c * P:(c + 1) * P], q_sb[i][:].bitcast(F32)[:, lo:lo + P], ident_f[:])
+
+        def keep_q(i, j, eng):
+            q_t[i, j] = qtpool.tile([P, NW * P], F32, name="q_t%d" % j, tag="q_t%d" % j)
+            copy_on(eng, q_t[i, j][:], qt_ps[i, j][:])
 
         def q_cols(i, k, j):
-            if WORDS:
-                view = q_t[i][:].bitcast(BF16).rearrange("p (c m e) -> p c m e", c=ND // 2, e=2)
-                return view[:, k // 2, j * P:(j + 1) * P, k % 2]
-            return q_t[i][:, k * T + j * P:k * T + (j + 1) * P]
+            view = q_t[i, j][:].bitcast(BF16).rearrange("p (c m e) -> p c m e", c=NW, e=2)
+            return view[:, k // 2, :, k % 2]
 
-        def scores(i, b):
-            s_ps[i, b] = psum.tile([P, NT, P], F32, name="s_ps", tag="S%d" % b)
-            for j in range(b + 1):
-                for k in range(ND):
-                    nc.tensor.matmul(
-                        s_ps[i, b][:, j, :],
-                        lhsT=q_cols(i, k, j),
-                        rhs=q_cols(i, k, b),
-                        start=(k == 0),
-                        stop=(k == ND - 1),
-                    )
+        def bank(i, b):
+            if (i, b) not in s_ps:
+                s_ps[i, b] = psum.tile([P, NT, P], F32, name="s_ps", tag="S%d" % b)
+            return s_ps[i, b]
+
+        def score_mm(i, b, j, k):
+            nc.tensor.matmul(
+                bank(i, b)[:, j, :],
+                lhsT=q_cols(i, k, j),
+                rhs=q_cols(i, k, b),
+                start=(k == 0),
+                stop=(k == ND - 1),
+            )
 
         def upper_out(i, b, eng):
             u_sb[i, b] = upool.tile([P, b, P], F32, name="u_sb%d" % b, tag="u_sb%d" % b)
             copy_on(eng, u_sb[i, b][:], s_ps[i, b][:, 0:b, :])
 
-        def mirror(i, tgt):
-            for src in range(NT - 1, tgt, -1):
-                nc.tensor.transpose(s_ps[i, tgt][:, src, :], u_sb[i, src][:, tgt, :], ident_f[:])
+        def mirror(i, src, tgt):
+            nc.tensor.transpose(bank(i, tgt)[:, src, :], u_sb[i, src][:, tgt, :], ident_f[:])
 
         def group_s(i, b, eng):
             if b == NT - 1:
@@ -152,13 +141,12 @@ def tile_linearattention_pa_t_kernel(tc, q_rot, v, out):
                 in_=s_grp[i][:, b].rearrange("p m j -> p (m j)"),
             )
 
-        def group_v(i, h, eng="dve"):
+        def group_v(i, h):
             if h == 0:
-                tag = "v_grp" if eng == "dve" else "v_grp_act"
-                v_grp[i] = vgpool.tile([P, D, NT], BF16, name=tag, tag=tag, align_bytes=64)
+                v_grp[i] = vgpool.tile([P, D, NT], BF16, name="v_grp", tag="v_grp", align_bytes=64)
             cols = slice(h * HALF, (h + 1) * HALF)
             copy_on(
-                eng,
+                "dve",
                 v_grp[i][:, cols, :].rearrange("p (c r) j -> p c j r", r=4),
                 v_sb[i][:, :, cols].rearrange("p j (c r) -> p c j r", r=4),
             )
@@ -172,7 +160,7 @@ def tile_linearattention_pa_t_kernel(tc, q_rot, v, out):
                 in_=v_grp[i][:].rearrange("p c j -> p (c j)"),
             )
 
-        def second(i, b, tags, engs):
+        def second(i, b, engs, tags=("O0", "O1")):
             if b == NT - 1:
                 o_sb[i] = opool.tile([P, NT, D], F32, name="o_sb", tag="o_sb")
             rows = slice(b * P, (b + 1) * P)
@@ -194,25 +182,44 @@ def tile_linearattention_pa_t_kernel(tc, q_rot, v, out):
                 cols = slice(h * HALF, (h + 1) * HALF)
                 copy_on(engs[h], o_sb[i][:, b, cols], accs[h][:])
 
-        def finish_scores(i):
-            group_s(i, 2, "dve")
-            group_s(i, 1, "dve")
-            quant_s(i, 2)
-            group_s(i, 0, "dve")
-            quant_s(i, 1)
-            quant_s(i, 0)
-
         def store(i, lo, hi):
             nc.sync.dma_start(out=ov[i][:, lo:hi, :], in_=o_sb[i][:, lo:hi, :])
 
         AA = ("act", "act")
+        AD = ("act", "dve")
+
+        def woven(i):
+            prev = i - 1
+            nxt = i + 1
+            side = [None] * N_SLOTS
+            if prev >= 0:
+                side[0] = (mirror, prev, 2, 1)
+                side[1] = (mirror, prev, 2, 0)
+                side[2] = (mirror, prev, 1, 0)
+            if nxt < NB:
+                places = (3, 4, 5, 6, 7, 8, 9, 10, 11, 12, 15, 16, 18, 19, 20, 21)
+                for n, place in enumerate(places):
+                    side[place] = (turn_q, nxt, J_ORDER[n // NW], n % NW, "T%d" % ((n // NW) % 2))
+                side[13] = (mirror, i, 3, 1)
+                side[14] = (mirror, i, 3, 0)
+                side[17] = (mirror, i, 3, 2)
+            return side
+
         load_q(0, True)
+        load_q(1, True)
         load_v(0)
-        for i in range(1, RING):
-            load_q(i, False)
-            load_v(i)
+        load_q(2, False)
+        load_v(1)
+        load_q(3, False)
+        load_v(2)
+        load_v(3)
         idle_pass(WARM_FIRST)
-        transpose_q(0, 2)
+        for n, j in enumerate(J_ORDER):
+            for c in range(NW):
+                turn_q(0, j, c, ("T0", "T1", "O0", "O1")[n])
+            if n < NT - 1:
+                idle_pass(2)
+            keep_q(0, j, "act" if n % 2 == 0 else "dve")
 
         for i in range(NB - 1):
             prev = i - 1
@@ -221,73 +228,123 @@ def tile_linearattention_pa_t_kernel(tc, q_rot, v, out):
                 load_q(i + RING, False)
             if prev >= 0 and prev + RING < NB:
                 load_v(prev + RING)
-            if i >= NB - 3:
-                group_v(NB - 1, i - (NB - 3), "act")
-            if prev >= 0:
-                finish_scores(prev)
-            if i == 0:
-                scores(i, 1)
-                upper_out(i, 1, "act")
-            scores(i, 3)
-            upper_out(i, 3, "act")
-            group_s(i, 3, "act")
-            if prev >= 0:
-                second(prev, 3, ("P0", "P1"), AA)
-                second(prev, 2, ("S1", "S0"), AA)
-                store(prev, 2, 4)
-            group_v(i, 0)
-            group_v(i, 1)
-            quant_s(i, 3)
-            scores(i, 2)
-            upper_out(i, 2, "act")
-            transpose_q(nxt)
-            if i > 0:
-                scores(i, 1)
-                upper_out(i, 1, "act")
-            if prev >= 0:
-                second(prev, 1, ("S3", "P2"), AA)
-                second(prev, 0, ("P3", "P0"), AA)
-                store(prev, 0, 2)
-            quant_v(i)
-            if i == NB - 2:
-                quant_v(NB - 1)
-            scores(i, 0)
-            mirror(i, 2)
-            mirror(i, 1)
-            mirror(i, 0)
+            side = woven(i)
+            done = 0
+            for b, j in GROUPS:
+                for k in range(ND):
+                    score_mm(i, b, j, k)
+                    done += 1
+                    if done == 32:
+                        upper_out(i, 3, "act")
+                        group_s(i, 3, "dve")
+                        if prev < 0:
+                            group_v(i, 0)
+                            group_v(i, 1)
+                        quant_v(i)
+                        quant_s(i, 3)
+                    if done == 56:
+                        upper_out(i, 2, "act")
+                    if done == 72:
+                        upper_out(i, 1, "act")
+                    if done in SLOT_AT:
+                        slot = SLOT_AT.index(done)
+                        if side[slot] is not None:
+                            side[slot][0](*side[slot][1:])
+                        if prev >= 0 and slot == 0:
+                            group_s(prev, 1, "dve")
+                            quant_s(prev, 2)
+                        if prev >= 0 and slot == 2:
+                            group_s(prev, 0, "dve")
+                            quant_s(prev, 1)
+                            group_v(i, 0)
+                            quant_s(prev, 0)
+                            group_v(i, 1)
+                        if slot == 6:
+                            keep_q(nxt, 3, "act")
+                        if slot == 10:
+                            keep_q(nxt, 0, "act")
+                        if slot == 16:
+                            keep_q(nxt, 1, "dve" if prev >= 0 else "act")
+                        if slot == 17:
+                            group_s(i, 2, "dve" if prev >= 0 else "act")
+                        if slot == 21:
+                            keep_q(nxt, 2, "act")
+                    if prev >= 0:
+                        if done == SLOT_AT[2] + 2:
+                            second(prev, 3, AA)
+                        if done == SLOT_AT[6] + 2:
+                            second(prev, 2, AA)
+                            store(prev, 2, 4)
+                        if done == SLOT_AT[11] + 2:
+                            second(prev, 1, AA)
+                        if done == SLOT_AT[16] + 2:
+                            second(prev, 0, AA)
+                            store(prev, 0, 2)
 
         i = NB - 1
         prev = i - 1
-        finish_scores(prev)
-        scores(i, 3)
-        second(prev, 3, ("P0", "P1"), AA)
-        second(prev, 2, ("S1", "S0"), ("dve", "dve"))
-        store(prev, 2, 4)
-        upper_out(i, 3, "act")
-        group_s(i, 3, "act")
-        scores(i, 2)
-        upper_out(i, 2, "dve")
-        quant_s(i, 3)
-        second(prev, 1, ("P2", "P3"), AA)
-        second(prev, 0, ("P0", "P1"), ("dve", "act"))
-        store(prev, 0, 2)
-        mirror(i, 2)
-        group_s(i, 2, "dve")
-        quant_s(i, 2)
-        scores(i, 1)
-        upper_out(i, 1, "dve")
-        second(i, 3, ("S3", "P2"), AA)
-        store(i, 3, 4)
-        mirror(i, 1)
+        done = 0
+        for b, j in LAST_GROUPS:
+            for k in range(ND):
+                score_mm(i, b, j, k)
+                done += 1
+                if done == 3:
+                    mirror(prev, 2, 1)
+                    group_s(prev, 1, "dve")
+                    quant_s(prev, 2)
+                if done == 7:
+                    mirror(prev, 2, 0)
+                if done == 10:
+                    mirror(prev, 1, 0)
+                    group_s(prev, 0, "dve")
+                    quant_s(prev, 1)
+                    group_v(i, 0)
+                    quant_s(prev, 0)
+                    group_v(i, 1)
+                    quant_v(i)
+                if done == 12:
+                    second(prev, 3, AA)
+                if done == 24:
+                    second(prev, 2, AA, ("T0", "T1"))
+                    store(prev, 2, 4)
+                if done == 32:
+                    upper_out(i, 3, "act")
+                    group_s(i, 3, "dve")
+                if done == 36:
+                    second(prev, 1, AA)
+                if done == 44:
+                    quant_s(i, 3)
+                    second(prev, 0, AD, ("T0", "T1"))
+                    store(prev, 0, 2)
+                if done == 50:
+                    mirror(i, 3, 1)
+                if done == 53:
+                    mirror(i, 3, 0)
+                if done == 56:
+                    upper_out(i, 2, "act")
+                if done == 59:
+                    mirror(i, 3, 2)
+                    group_s(i, 2, "dve")
+                if done == 62:
+                    second(i, 3, AA)
+                    store(i, 3, 4)
+                if done == 64:
+                    upper_out(i, 1, "dve")
+                    quant_s(i, 2)
+                if done == 68:
+                    mirror(i, 2, 1)
+                if done == 71:
+                    second(i, 2, AD, ("T0", "T1"))
+                    store(i, 2, 3)
+                if done == 74:
+                    mirror(i, 2, 0)
+                if done == 77:
+                    mirror(i, 1, 0)
+                    group_s(i, 0, "act")
         group_s(i, 1, "dve")
-        quant_s(i, 1)
-        second(i, 2, ("P3", "P0"), AA)
-        store(i, 2, 3)
-        scores(i, 0)
-        mirror(i, 0)
-        group_s(i, 0, "dve")
         quant_s(i, 0)
-        second(i, 1, ("P1", "S3"), AA)
-        store(i, 1, 2)
-        second(i, 0, ("S2", "S1"), ("act", "dve"))
+        quant_s(i, 1)
+        second(i, 0, AD, ("S3", "S2"))
         store(i, 0, 1)
+        second(i, 1, AD)
+        store(i, 1, 2)

@@ -24,6 +24,7 @@ WARM_N = 256
 WARM_FIRST = 7
 J_ORDER = (3, 0, 1, 2)
 GROUPS = tuple((b, j) for b in (3, 2, 1, 0) for j in range(b + 1))
+FIRST_GROUPS = ((3, 3),) + GROUPS[0:3] + GROUPS[4:]
 LAST_GROUPS = GROUPS[0:8] + ((0, 0), (1, 1))
 N_MM = len(GROUPS) * ND
 N_SLOTS = 22
@@ -160,7 +161,7 @@ def tile_linearattention_pa_t_kernel(tc, q_rot, v, out):
                 in_=v_grp[i][:].rearrange("p c j -> p (c j)"),
             )
 
-        def second(i, b, engs, tags=("O0", "O1")):
+        def second(i, b, engs, tags=("O0", "O1"), halves=False):
             if b == NT - 1:
                 o_sb[i] = opool.tile([P, NT, D], F32, name="o_sb", tag="o_sb")
             rows = slice(b * P, (b + 1) * P)
@@ -181,6 +182,8 @@ def tile_linearattention_pa_t_kernel(tc, q_rot, v, out):
             for h in range(2):
                 cols = slice(h * HALF, (h + 1) * HALF)
                 copy_on(engs[h], o_sb[i][:, b, cols], accs[h][:])
+                if halves:
+                    nc.sync.dma_start(out=ov[i][:, b, cols], in_=o_sb[i][:, b, cols])
 
         def store(i, lo, hi):
             nc.sync.dma_start(out=ov[i][:, lo:hi, :], in_=o_sb[i][:, lo:hi, :])
@@ -197,12 +200,12 @@ def tile_linearattention_pa_t_kernel(tc, q_rot, v, out):
                 side[1] = (mirror, prev, 2, 0)
                 side[2] = (mirror, prev, 1, 0)
             if nxt < NB:
-                places = (3, 4, 5, 6, 7, 8, 9, 10, 11, 12, 15, 16, 18, 19, 20, 21)
+                places = (3, 4, 5, 6, 7, 8, 9, 10, 11, 12, 16, 17, 18, 19, 20, 21)
                 for n, place in enumerate(places):
                     side[place] = (turn_q, nxt, J_ORDER[n // NW], n % NW, "T%d" % ((n // NW) % 2))
                 side[13] = (mirror, i, 3, 1)
                 side[14] = (mirror, i, 3, 0)
-                side[17] = (mirror, i, 3, 2)
+                side[15] = (mirror, i, 3, 2)
             return side
 
         load_q(0, True)
@@ -214,26 +217,32 @@ def tile_linearattention_pa_t_kernel(tc, q_rot, v, out):
         load_v(2)
         load_v(3)
         idle_pass(WARM_FIRST)
-        for n, j in enumerate(J_ORDER):
+        for n, j in enumerate(J_ORDER[0:3]):
             for c in range(NW):
-                turn_q(0, j, c, ("T0", "T1", "O0", "O1")[n])
-            if n < NT - 1:
+                turn_q(0, j, c, ("T0", "T1", "O0")[n])
+            if n < 2:
                 idle_pass(2)
             keep_q(0, j, "act" if n % 2 == 0 else "dve")
 
         for i in range(NB - 1):
             prev = i - 1
             nxt = i + 1
-            if i + RING < NB:
+            if prev >= 0 and i + RING < NB:
                 load_q(i + RING, False)
             if prev >= 0 and prev + RING < NB:
                 load_v(prev + RING)
             side = woven(i)
+            mx_after = (2, 8, 13, 19) if prev != 0 else (8, 13, 16, 19)
             done = 0
-            for b, j in GROUPS:
+            for b, j in GROUPS if prev >= 0 else FIRST_GROUPS:
                 for k in range(ND):
                     score_mm(i, b, j, k)
                     done += 1
+                    if prev < 0 and done == ND:
+                        for c in range(NW):
+                            turn_q(0, J_ORDER[3], c, "O1")
+                        keep_q(0, J_ORDER[3], "dve")
+                        load_q(RING, False)
                     if done == 32:
                         upper_out(i, 3, "act")
                         group_s(i, 3, "dve")
@@ -242,8 +251,6 @@ def tile_linearattention_pa_t_kernel(tc, q_rot, v, out):
                             group_v(i, 1)
                         quant_v(i)
                         quant_s(i, 3)
-                    if done == 56:
-                        upper_out(i, 2, "act")
                     if done == 72:
                         upper_out(i, 1, "act")
                     if done in SLOT_AT:
@@ -263,21 +270,22 @@ def tile_linearattention_pa_t_kernel(tc, q_rot, v, out):
                             keep_q(nxt, 3, "act")
                         if slot == 10:
                             keep_q(nxt, 0, "act")
-                        if slot == 16:
-                            keep_q(nxt, 1, "dve" if prev >= 0 else "act")
-                        if slot == 17:
+                        if slot == 15:
+                            upper_out(i, 2, "act")
                             group_s(i, 2, "dve" if prev >= 0 else "act")
+                        if slot == 17:
+                            keep_q(nxt, 1, "act")
                         if slot == 21:
-                            keep_q(nxt, 2, "act")
+                            keep_q(nxt, 2, "dve" if prev >= 0 else "act")
                     if prev >= 0:
-                        if done == SLOT_AT[2] + 2:
+                        if done == SLOT_AT[mx_after[0]] + 2:
                             second(prev, 3, AA)
-                        if done == SLOT_AT[6] + 2:
+                        if done == SLOT_AT[mx_after[1]] + 2:
                             second(prev, 2, AA)
                             store(prev, 2, 4)
-                        if done == SLOT_AT[11] + 2:
+                        if done == SLOT_AT[mx_after[2]] + 2:
                             second(prev, 1, AA)
-                        if done == SLOT_AT[16] + 2:
+                        if done == SLOT_AT[mx_after[3]] + 2:
                             second(prev, 0, AA)
                             store(prev, 0, 2)
 
@@ -320,10 +328,9 @@ def tile_linearattention_pa_t_kernel(tc, q_rot, v, out):
                     mirror(i, 3, 1)
                 if done == 53:
                     mirror(i, 3, 0)
-                if done == 56:
-                    upper_out(i, 2, "act")
-                if done == 59:
+                if done == 58:
                     mirror(i, 3, 2)
+                    upper_out(i, 2, "act")
                     group_s(i, 2, "dve")
                 if done == 62:
                     second(i, 3, AA)
@@ -338,13 +345,11 @@ def tile_linearattention_pa_t_kernel(tc, q_rot, v, out):
                     store(i, 2, 3)
                 if done == 74:
                     mirror(i, 2, 0)
-                if done == 77:
+                if done == 76:
                     mirror(i, 1, 0)
                     group_s(i, 0, "act")
         group_s(i, 1, "dve")
         quant_s(i, 0)
         quant_s(i, 1)
-        second(i, 0, AD, ("S3", "S2"))
-        store(i, 0, 1)
-        second(i, 1, AD)
-        store(i, 1, 2)
+        second(i, 0, AD, ("S3", "S2"), True)
+        second(i, 1, AD, ("O0", "O1"), True)

@@ -51,6 +51,8 @@ def tile_linearattention_pa_t_kernel(tc, q_rot, v, out):
 
         ident_f = const.tile([P, P], F32, name="ident_f", tag="ident_f")
         make_identity(nc, ident_f[:])
+        ident_b = const.tile([P, P], BF16, name="ident_b", tag="ident_b")
+        make_identity(nc, ident_b[:])
 
         warm = const.tile([P, HALF], BF16, name="warm", tag="warm")
         nc.vector.memset(warm[:].bitcast(I32), 0)
@@ -94,17 +96,17 @@ def tile_linearattention_pa_t_kernel(tc, q_rot, v, out):
 
         def turn_q(i, j, c, tag):
             if c == 0:
-                qt_ps[i, j] = psum.tile([P, NW * P], F32, name="qt_ps", tag=tag)
-            lo = j * (D // 2) + c * P
-            nc.tensor.transpose(qt_ps[i, j][:, c * P:(c + 1) * P], q_sb[i][:].bitcast(F32)[:, lo:lo + P], ident_f[:])
+                qt_ps[i, j] = psum.tile([P, ND * P], BF16, name="qt_ps", tag=tag)
+            for k in (2 * c, 2 * c + 1):
+                lo = j * D + k * P
+                nc.tensor.transpose(qt_ps[i, j][:, k * P:(k + 1) * P], q_sb[i][:, lo:lo + P], ident_b[:])
 
         def keep_q(i, j, eng):
-            q_t[i, j] = qtpool.tile([P, NW * P], F32, name="q_t%d" % j, tag="q_t%d" % j)
+            q_t[i, j] = qtpool.tile([P, ND * P], BF16, name="q_t%d" % j, tag="q_t%d" % j)
             copy_on(eng, q_t[i, j][:], qt_ps[i, j][:])
 
         def q_cols(i, k, j):
-            view = q_t[i, j][:].bitcast(BF16).rearrange("p (c m e) -> p c m e", c=NW, e=2)
-            return view[:, k // 2, :, k % 2]
+            return q_t[i, j][:, k * P:(k + 1) * P]
 
         def bank(i, b):
             if (i, b) not in s_ps:

@@ -163,6 +163,16 @@ def tile_linearattention_pa_t_kernel(tc, q_rot, v, out):
                 in_=v_grp[i][:].rearrange("p c j -> p (c j)"),
             )
 
+        v_queue = [(step, i) for i in range(1, NB) for step in (0, 1, 2)]
+
+        def v_steps(n):
+            for r in range(n):
+                step, i = v_queue.pop(0)
+                if step < 2:
+                    group_v(i, step)
+                else:
+                    quant_v(i)
+
         def second(i, b, engs, tags=("O0", "O1"), halves=False):
             if b == NT - 1:
                 o_sb[i] = opool.tile([P, NT, D], F32, name="o_sb", tag="o_sb")
@@ -251,8 +261,13 @@ def tile_linearattention_pa_t_kernel(tc, q_rot, v, out):
                         if prev < 0:
                             group_v(i, 0)
                             group_v(i, 1)
-                        quant_v(i)
+                            quant_v(i)
+                        else:
+                            v_steps(1)
                         quant_s(i, 3)
+                        if prev >= 0:
+                            v_steps(i % 2)
+
                     if done == 72:
                         upper_out(i, 1, "act")
                     if done in SLOT_AT:
@@ -265,9 +280,9 @@ def tile_linearattention_pa_t_kernel(tc, q_rot, v, out):
                         if prev >= 0 and slot == 2:
                             group_s(prev, 0, "dve")
                             quant_s(prev, 1)
-                            group_v(i, 0)
+                            v_steps(1)
                             quant_s(prev, 0)
-                            group_v(i, 1)
+                            v_steps(1)
                         if slot == 6:
                             keep_q(nxt, 3, "act")
                         if slot == 10:
@@ -308,10 +323,7 @@ def tile_linearattention_pa_t_kernel(tc, q_rot, v, out):
                     mirror(prev, 1, 0)
                     group_s(prev, 0, "dve")
                     quant_s(prev, 1)
-                    group_v(i, 0)
                     quant_s(prev, 0)
-                    group_v(i, 1)
-                    quant_v(i)
                 if done == 12:
                     second(prev, 3, AA)
                 if done == 24:

@@ -132,8 +132,8 @@ def tile_linearattention_pa_t_kernel(tc, q_rot, v, out):
         def group_s(i, b, eng):
             if b == NT - 1:
                 s_grp[i] = mxpool.tile([P, NT, P, NT], BF16, name="s_grp", tag="s_grp", align_bytes=64)
-                s_cod[i] = mxpool.tile([P, T], U32, name="s_cod", tag="s_cod", align_bytes=64)
-                s_scl[i] = mxpool.tile([P, T], U8, name="s_scl", tag="s_scl", align_bytes=64)
+                s_cod[i] = mxpool.tile([P, T], U32, name="s_cod", tag="s_cod", align_bytes=256)
+                s_scl[i] = mxpool.tile([P, 64 + T], U8, name="s_scl", tag="s_scl", align_bytes=256)[:, 64:64 + T]
             copy_on(eng, s_grp[i][:, b], s_ps[i, b][:].rearrange("p j m -> p m j"))
 
         def quant_s(i, b):
@@ -155,8 +155,8 @@ def tile_linearattention_pa_t_kernel(tc, q_rot, v, out):
             )
 
         def quant_v(i):
-            v_cod[i] = mxpool.tile([P, D], U32, name="v_cod", tag="v_cod", align_bytes=64, bufs=3)
-            v_scl[i] = mxpool.tile([P, D], U8, name="v_scl", tag="v_scl", align_bytes=64, bufs=3)
+            v_cod[i] = mxpool.tile([P, 32 + D], U32, name="v_cod", tag="v_cod", align_bytes=256, bufs=3)[:, 32:32 + D]
+            v_scl[i] = mxpool.tile([P, 192 + D], U8, name="v_scl", tag="v_scl", align_bytes=256, bufs=3)[:, 192:192 + D]
             nc.vector.quantize_mx(
                 out=v_cod[i][:].bitcast(FP8X4),
                 scales=v_scl[i][:],

@@ -244,7 +244,7 @@ def tile_linearattention_pa_t_kernel(tc, q_rot, v, out):
             if prev >= 0 and prev + RING < NB:
                 load_v(prev + RING)
             side = woven(i)
-            mx_after = (2, 8, 13, 19) if prev != 0 else (8, 13, 16, 19)
+            mx_after = (2, 8, 13, 19) if prev != 0 else (8, 12, 16, 20)
             done = 0
             for b, j in GROUPS if prev >= 0 else FIRST_GROUPS:
                 for k in range(ND):
@@ -270,6 +270,8 @@ def tile_linearattention_pa_t_kernel(tc, q_rot, v, out):
 
                     if done == 72:
                         upper_out(i, 1, "act")
+                        if prev < 0:
+                            group_s(i, 2, "act")
                     if done in SLOT_AT:
                         slot = SLOT_AT.index(done)
                         if side[slot] is not None:
@@ -289,11 +291,12 @@ def tile_linearattention_pa_t_kernel(tc, q_rot, v, out):
                             keep_q(nxt, 0, "act")
                         if slot == 15:
                             upper_out(i, 2, "act")
-                            group_s(i, 2, "dve" if prev >= 0 else "act")
+                            if prev >= 0:
+                                group_s(i, 2, "dve")
                         if slot == 17:
                             keep_q(nxt, 1, "act")
                         if slot == 21:
-                            keep_q(nxt, 2, "dve" if prev >= 0 else "act")
+                            keep_q(nxt, 2, "dve" if i % 2 == 0 and prev >= 0 else "act")
                     if prev >= 0:
                         if done == SLOT_AT[mx_after[0]] + 2:
                             second(prev, 3, AA)

from contextlib import ExitStack

import concourse.mybir as mybir
from concourse.masks import make_identity

F32 = mybir.dt.float32
BF16 = mybir.dt.bfloat16
U32 = mybir.dt.uint32
U8 = mybir.dt.uint8
I32 = mybir.dt.int32
FP8X4 = mybir.dt.float8_e4m3fn_x4

NB = 8
T = 512
D = 1024
P = 128
NT = T // P
ND = D // P
NW = ND // 2
HALF = 512
FLOPS = 2 * NB * T * T * D * 2
RING = 4
WARM_N = 256
WARM_FIRST = 7
J_ORDER = (3, 0, 1, 2)
GROUPS = tuple((b, j) for b in (3, 2, 1, 0) for j in range(b + 1))
FIRST_GROUPS = ((3, 3),) + GROUPS[0:3] + GROUPS[4:]
LAST_GROUPS = GROUPS[0:8] + ((0, 0), (1, 1))
N_MM = len(GROUPS) * ND
N_SLOTS = 22
SLOT_AT = tuple((n + 1) * N_MM // N_SLOTS for n in range(N_SLOTS))


def tile_linearattention_pa_t_kernel(tc, q_rot, v, out):
    nc = tc.nc
    qv = q_rot.rearrange("b h (p j) d -> (b h) p (j d)", j=NT)
    vv = v.rearrange("b h (p j) d -> (b h) p j d", j=NT)
    ov = out.rearrange("b h (p j) d -> (b h) p j d", j=NT)

    with ExitStack() as ctx:
        ctx.enter_context(tc.manual_schedule())
        const = ctx.enter_context(tc.tile_pool(name="const", bufs=1))
        qpool = ctx.enter_context(tc.tile_pool(name="qpool", bufs=RING))
        vpool = ctx.enter_context(tc.tile_pool(name="vpool", bufs=RING))
        qtpool = ctx.enter_context(tc.tile_pool(name="qtpool", bufs=2))
        vgpool = ctx.enter_context(tc.tile_pool(name="vgpool", bufs=1))
        mxpool = ctx.enter_context(tc.tile_pool(name="mxpool", bufs=2))
        upool = ctx.enter_context(tc.tile_pool(name="upool", bufs=2))
        opool = ctx.enter_context(tc.tile_pool(name="opool", bufs=3))
        psum = ctx.enter_context(tc.psum_pool(name="psum", bufs=1))

        ident_f = const.tile([P, P], F32, name="ident_f", tag="ident_f")
        make_identity(nc, ident_f[:])
        ident_b = const.tile([P, P], BF16, name="ident_b", tag="ident_b")
        make_identity(nc, ident_b[:])

        warm = const.tile([P, HALF], BF16, name="warm", tag="warm")
        nc.vector.memset(warm[:].bitcast(I32), 0)
        warm_ps = psum.tile([P, HALF], F32, name="warm_ps", tag="S0")

        def idle_pass(n):
            for r in range(n):
                nc.tensor.matmul(warm_ps[:, 0:WARM_N], lhsT=warm[:, 0:P], rhs=warm[:, 0:WARM_N], start=True, stop=True)

        q_sb = {}
        v_sb = {}
        qt_ps = {}
        q_t = {}
        s_ps = {}
        u_sb = {}
        s_grp = {}
        s_cod = {}
        s_scl = {}
        v_grp = {}
        v_cod = {}
        v_scl = {}
        o_sb = {}

        def copy_on(eng, dst, src):
            if eng == "act":
                nc.scalar.copy(out=dst, in_=src)
            else:
                nc.vector.tensor_copy(out=dst, in_=src)

        def load_q(i, parts):
            q_sb[i] = qpool.tile([P, NT * D], BF16, name="q_sb", tag="q_sb")
            if parts:
                for j in J_ORDER:
                    nc.sync.dma_start(out=q_sb[i][:, j * D:(j + 1) * D], in_=qv[i][:, j * D:(j + 1) * D])
            else:
                nc.sync.dma_start(out=q_sb[i][:], in_=qv[i])

        def load_v(i):
            v_sb[i] = vpool.tile([P, NT, D], BF16, name="v_sb", tag="v_sb")
            nc.sync.dma_start(out=v_sb[i][:], in_=vv[i])

        def turn_q(i, j, c, tag):
            if c == 0:
                qt_ps[i, j] = psum.tile([P, ND * P], BF16, name="qt_ps", tag=tag)
            for k in (2 * c, 2 * c + 1):
                lo = j * D + k * P
                nc.tensor.transpose(qt_ps[i, j][:, k * P:(k + 1) * P], q_sb[i][:, lo:lo + P], ident_b[:])

        def keep_q(i, j, eng):
            q_t[i, j] = qtpool.tile([P, ND * P], BF16, name="q_t%d" % j, tag="q_t%d" % j)
            copy_on(eng, q_t[i, j][:], qt_ps[i, j][:])

        def q_cols(i, k, j):
            return q_t[i, j][:, k * P:(k + 1) * P]

        def bank(i, b):
            if (i, b) not in s_ps:
                s_ps[i, b] = psum.tile([P, NT, P], F32, name="s_ps", tag="S%d" % b)
            return s_ps[i, b]

        def score_mm(i, b, j, k):
            nc.tensor.matmul(
                bank(i, b)[:, j, :],
                lhsT=q_cols(i, k, j),
                rhs=q_cols(i, k, b),
                start=(k == 0),
                stop=(k == ND - 1),
            )

        def upper_out(i, b, eng):
            u_sb[i, b] = upool.tile([P, b, P], F32, name="u_sb%d" % b, tag="u_sb%d" % b)
            copy_on(eng, u_sb[i, b][:], s_ps[i, b][:, 0:b, :])

        def mirror(i, src, tgt):
            nc.tensor.transpose(bank(i, tgt)[:, src, :], u_sb[i, src][:, tgt, :], ident_f[:])

        def group_s(i, b, eng):
            if b == NT - 1:
                s_grp[i] = mxpool.tile([P, NT, P, NT], BF16, name="s_grp", tag="s_grp", align_bytes=64)
                s_cod[i] = mxpool.tile([P, T], U32, name="s_cod", tag="s_cod", align_bytes=256)
                s_scl[i] = mxpool.tile([P, 64 + T], U8, name="s_scl", tag="s_scl", align_bytes=256)[:, 64:64 + T]
            copy_on(eng, s_grp[i][:, b], s_ps[i, b][:].rearrange("p j m -> p m j"))

        def quant_s(i, b):
            cols = slice(b * P, (b + 1) * P)
            nc.vector.quantize_mx(
                out=s_cod[i][:, cols].bitcast(FP8X4),
                scales=s_scl[i][:, cols],
                in_=s_grp[i][:, b].rearrange("p m j -> p (m j)"),
            )

        def group_v(i, h):
            if h == 0:
                v_grp[i] = vgpool.tile([P, D, NT], BF16, name="v_grp", tag="v_grp", align_bytes=64)
            cols = slice(h * HALF, (h + 1) * HALF)
            copy_on(
                "dve",
                v_grp[i][:, cols, :].rearrange("p (c r) j -> p c j r", r=4),
                v_sb[i][:, :, cols].rearrange("p j (c r) -> p c j r", r=4),
            )

        def quant_v(i):
            v_cod[i] = mxpool.tile([P, 32 + D], U32, name="v_cod", tag="v_cod", align_bytes=256, bufs=3)[:, 32:32 + D]
            v_scl[i] = mxpool.tile([P, 192 + D], U8, name="v_scl", tag="v_scl", align_bytes=256, bufs=3)[:, 192:192 + D]
            nc.vector.quantize_mx(
                out=v_cod[i][:].bitcast(FP8X4),
                scales=v_scl[i][:],
                in_=v_grp[i][:].rearrange("p c j -> p (c j)"),
            )

        v_queue = [(step, i) for i in range(1, NB) for step in (0, 1, 2)]

        def v_steps(n):
            for r in range(n):
                step, i = v_queue.pop(0)
                if step < 2:
                    group_v(i, step)
                else:
                    quant_v(i)

        def second(i, b, engs, tags=("O0", "O1"), halves=False):
            if b == NT - 1:
                o_sb[i] = opool.tile([P, NT, D], F32, name="o_sb", tag="o_sb")
            rows = slice(b * P, (b + 1) * P)
            accs = []
            for h in range(2):
                cols = slice(h * HALF, (h + 1) * HALF)
                acc = psum.tile([P, HALF], F32, name="o_ps", tag=tags[h])
                nc.tensor.matmul_mx(
                    out=acc[:],
                    lhsT=s_cod[i][:, rows].bitcast(FP8X4),
                    lhsT_scale=s_scl[i][:, rows],
                    rhs=v_cod[i][:, cols].bitcast(FP8X4),
                    rhs_scale=v_scl[i][:, cols],
                    start=True,
                    stop=True,
                )
                accs.append(acc)
            for h in range(2):
                cols = slice(h * HALF, (h + 1) * HALF)
                copy_on(engs[h], o_sb[i][:, b, cols], accs[h][:])
                if halves:
                    nc.sync.dma_start(out=ov[i][:, b, cols], in_=o_sb[i][:, b, cols])

        def store(i, lo, hi):
            nc.sync.dma_start(out=ov[i][:, lo:hi, :], in_=o_sb[i][:, lo:hi, :])

        AA = ("act", "act")
        AD = ("act", "dve")

        def woven(i):
            prev = i - 1
            nxt = i + 1
            side = [None] * N_SLOTS
            if prev >= 0:
                side[0] = (mirror, prev, 2, 1)
                side[1] = (mirror, prev, 2, 0)
                side[2] = (mirror, prev, 1, 0)
            if nxt < NB:
                places = (3, 4, 5, 6, 7, 8, 9, 10, 11, 12, 16, 17, 18, 19, 20, 21)
                for n, place in enumerate(places):
                    side[place] = (turn_q, nxt, J_ORDER[n // NW], n % NW, "T%d" % ((n // NW) % 2))
                side[13] = (mirror, i, 3, 1)
                side[14] = (mirror, i, 3, 0)
                side[15] = (mirror, i, 3, 2)
            return side

        load_q(0, True)
        load_q(1, True)
        load_v(0)
        load_q(2, False)
        load_v(1)
        load_q(3, False)
        load_v(2)
        load_v(3)
        idle_pass(WARM_FIRST)
        for n, j in enumerate(J_ORDER[0:3]):
            for c in range(NW):
                turn_q(0, j, c, ("T0", "T1", "O0")[n])
            if n < 2:
                idle_pass(2)
            keep_q(0, j, "act" if n % 2 == 0 else "dve")

        for i in range(NB - 1):
            prev = i - 1
            nxt = i + 1
            if prev >= 0 and i + RING < NB:
                load_q(i + RING, False)
            if prev >= 0 and prev + RING < NB:
                load_v(prev + RING)
            side = woven(i)
            mx_after = (2, 8, 13, 19) if prev != 0 else (8, 12, 16, 20)
            done = 0
            for b, j in GROUPS if prev >= 0 else FIRST_GROUPS:
                for k in range(ND):
                    score_mm(i, b, j, k)
                    done += 1
                    if prev < 0 and done == ND:
                        for c in range(NW):
                            turn_q(0, J_ORDER[3], c, "O1")
                        keep_q(0, J_ORDER[3], "dve")
                        load_q(RING, False)
                    if done == 32:
                        upper_out(i, 3, "act")
                        group_s(i, 3, "dve")
                        if prev < 0:
                            group_v(i, 0)
                            group_v(i, 1)
                            quant_v(i)
                        else:
                            v_steps(1)
                        quant_s(i, 3)
                        if prev >= 0:
                            v_steps(i % 2)

                    if done == 72:
                        upper_out(i, 1, "act")
                        if prev < 0:
                            group_s(i, 2, "act")
                    if done in SLOT_AT:
                        slot = SLOT_AT.index(done)
                        if side[slot] is not None:
                            side[slot][0](*side[slot][1:])
                        if prev >= 0 and slot == 0:
                            group_s(prev, 1, "dve")
                            quant_s(prev, 2)
                        if prev >= 0 and slot == 2:
                            group_s(prev, 0, "dve")
                            quant_s(prev, 1)
                            v_steps(1)
                            quant_s(prev, 0)
                            v_steps(1)
                        if slot == 6:
                            keep_q(nxt, 3, "act")
                        if slot == 10:
                            keep_q(nxt, 0, "act")
                        if slot == 15:
                            upper_out(i, 2, "act")
                            if prev >= 0:
                                group_s(i, 2, "dve")
                        if slot == 17:
                            keep_q(nxt, 1, "act")
                        if slot == 21:
                            keep_q(nxt, 2, "dve" if i % 2 == 0 and prev >= 0 else "act")
                    if prev >= 0:
                        if done == SLOT_AT[mx_after[0]] + 2:
                            second(prev, 3, AA)
                        if done == SLOT_AT[mx_after[1]] + 2:
                            second(prev, 2, AA)
                            store(prev, 2, 4)
                        if done == SLOT_AT[mx_after[2]] + 2:
                            second(prev, 1, AA)
                        if done == SLOT_AT[mx_after[3]] + 2:
                            second(prev, 0, AA)
                            store(prev, 0, 2)

        i = NB - 1
        prev = i - 1
        done = 0
        for b, j in LAST_GROUPS:
            for k in range(ND):
                score_mm(i, b, j, k)
                done += 1
                if done == 3:
                    mirror(prev, 2, 1)
                    group_s(prev, 1, "dve")
                    quant_s(prev, 2)
                if done == 7:
                    mirror(prev, 2, 0)
                if done == 10:
                    mirror(prev, 1, 0)
                    group_s(prev, 0, "dve")
                    quant_s(prev, 1)
                    quant_s(prev, 0)
                if done == 12:
                    second(prev, 3, AA)
                if done == 24:
                    second(prev, 2, AA, ("T0", "T1"))
                    store(prev, 2, 4)
                if done == 32:
                    upper_out(i, 3, "act")
                    group_s(i, 3, "dve")
                if done == 36:
                    second(prev, 1, AA)
                if done == 44:
                    quant_s(i, 3)
                    second(prev, 0, AD, ("T0", "T1"))
                    store(prev, 0, 2)
                if done == 50:
                    mirror(i, 3, 1)
                if done == 53:
                    mirror(i, 3, 0)
                if done == 58:
                    mirror(i, 3, 2)
                    upper_out(i, 2, "act")
                    group_s(i, 2, "dve")
                if done == 62:
                    second(i, 3, AA)
                    store(i, 3, 4)
                if done == 64:
                    upper_out(i, 1, "dve")
                    quant_s(i, 2)
                if done == 68:
                    mirror(i, 2, 1)
                if done == 71:
                    second(i, 2, AD, ("T0", "T1"))
                    store(i, 2, 3)
                if done == 74:
                    mirror(i, 2, 0)
                if done == 76:
                    mirror(i, 1, 0)
                    group_s(i, 0, "act")
        group_s(i, 1, "dve")
        quant_s(i, 0)
        quant_s(i, 1)
        second(i, 0, AD, ("S3", "S2"), True)
        second(i, 1, AD, ("O0", "O1"), True)
